import numpy as np
import ml_dtypes


def mxq(x, axis, fmt="e4m3"):
    dtype, down = {"e4m3": (ml_dtypes.float8_e4m3fn, 7), "e5m2": (ml_dtypes.float8_e5m2, 14)}[fmt]
    v = np.moveaxis(np.asarray(x, np.float32).astype(ml_dtypes.bfloat16).astype(np.float64), axis, -1)
    blocks = v.reshape(v.shape[:-1] + (-1, 32))
    amax = np.abs(blocks).max(-1, keepdims=True)
    byte = np.maximum(np.where(amax > 0, np.frexp(amax)[1] - 1 + 127, 0) - down, 1)
    scale = np.exp2(byte - 127.0)
    codes = (blocks / scale).astype(np.float32).astype(dtype).astype(np.float64)
    return np.moveaxis((codes * scale).reshape(v.shape), -1, axis)


WIDE = False


def mx_kscale(k):
    if not WIDE:
        return np.ones(k)
    levels = np.array([10, -10, 5, -5, 0])
    a = np.random.permutation(np.resize(levels, k // 512 * 4)).reshape(k // 512, 4)
    idx = np.arange(k)
    return np.exp2(a[idx // 512, idx % 128 // 32])


BF16 = ml_dtypes.bfloat16


def bf(x):
    return np.asarray(x, np.float32).astype(BF16)


def f64(x):
    return np.asarray(x).astype(np.float64)


B, D_IN, H, D_OUT = 8192, 4096, 512, 128
H2 = 2 * H
LN_EPS = 1e-5


def setup_inputs():
    s = mx_kscale(H)
    t = mx_kscale(H2)
    return {
        "h1": bf(np.tanh(np.random.standard_normal((B, H))) * s),
        "W_ih1": bf(np.random.standard_normal((H, H)) / np.sqrt(H) / s[None, :]),
        "b_ih1": bf(0.25 + 0.3 * np.random.standard_normal(H)),
        "b_hh1": bf(0.3 * np.random.standard_normal(H)),
        "ln_g": bf((1.0 + 0.1 * np.random.standard_normal(H2)) * t),
        "ln_b": bf(0.2 * np.random.standard_normal(H2) * t),
        "fc_W": bf(np.random.standard_normal((D_OUT, H2)) / np.sqrt(H2) / t[None, :]),
        "fc_b": bf(0.3 * np.random.standard_normal(D_OUT)),
    }


def reference(h1, W_ih1, b_ih1, b_hh1, ln_g, ln_b, fc_W, fc_b):
    h2 = np.tanh((mxq(f64(h1), 1, "e4m3") @ mxq(f64(W_ih1), 1, "e4m3").T) + f64(b_ih1) + f64(b_hh1))
    combined = np.concatenate([h2, h2], axis=1)
    mu = combined.mean(axis=-1, keepdims=True)
    var = combined.var(axis=-1, keepdims=True)
    normed = (combined - mu) / np.sqrt(var + LN_EPS) * f64(ln_g) + f64(ln_b)
    return (mxq(normed, 1, "e4m3") @ mxq(f64(fc_W), 1, "e4m3").T) + f64(fc_b)

@@ -1,0 +1,362 @@
+from contextlib import ExitStack
+
+from concourse import mybir
+from concourse.masks import make_identity
+
+F32 = mybir.dt.float32
+BF16 = mybir.dt.bfloat16
+U32 = mybir.dt.uint32
+U8 = mybir.dt.uint8
+FP8X4 = mybir.dt.float8_e4m3fn_x4
+ACT = mybir.ActivationFunctionType
+ALU = mybir.AluOpType
+
+P = 128
+B, H, H2, D_OUT = 8192, 512, 1024, 128
+LN_EPS = 1e-5
+ROW_TILES = 4
+BLOCK = P * ROW_TILES
+N_BLOCKS = B // BLOCK
+FLOPS = 2 * B * H * H + 2 * B * H2 * D_OUT
+MANUAL = True
+XH_ON_GPSIMD = True
+
+
+def tile_rnnclassifier_pa_t_kernel(
+    tc, h1, W_ih1, b_ih1, b_hh1, ln_g, ln_b, fc_W, fc_b, out
+):
+    nc = tc.nc
+    with ExitStack() as stack:
+        if MANUAL:
+            stack.enter_context(tc.manual_schedule())
+        const = stack.enter_context(tc.tile_pool(name="const", bufs=1))
+        h1pool = stack.enter_context(tc.tile_pool(name="h1pool", bufs=N_BLOCKS))
+        work = stack.enter_context(tc.tile_pool(name="work", bufs=2))
+        acts = stack.enter_context(tc.tile_pool(name="acts", bufs=8))
+        small = stack.enter_context(tc.tile_pool(name="small", bufs=4))
+        psum = stack.enter_context(tc.psum_pool(name="psum", bufs=1))
+
+        w_sb = const.tile([P, 4 * H], BF16)
+        nc.sync.dma_start(
+            out=w_sb[:].rearrange("p (t k) -> p t k", t=4),
+            in_=W_ih1.rearrange("(t p) k -> p t k", p=P),
+        )
+        h1_tiles = []
+        for blk in range(N_BLOCKS):
+            h1_sb = h1pool.tile([P, ROW_TILES * H], BF16, name="h1_sb")
+            nc.sync.dma_start(
+                out=h1_sb[:],
+                in_=h1[blk * BLOCK : (blk + 1) * BLOCK, :].rearrange(
+                    "(p i) k -> p (i k)", i=ROW_TILES
+                ),
+            )
+            h1_tiles.append(h1_sb)
+        b1_bc = const.tile([P, H], BF16)
+        nc.scalar.dma_start(out=b1_bc[:], in_=b_ih1.partition_broadcast(P))
+        b2_bc = const.tile([P, H], BF16)
+        nc.scalar.dma_start(out=b2_bc[:], in_=b_hh1.partition_broadcast(P))
+        gb_rows = const.tile([P, P], BF16)
+        nc.vector.memset(gb_rows[:], 0.0)
+        nc.scalar.dma_start(out=gb_rows[0:8, :], in_=ln_g.rearrange("(c p) -> c p", p=P))
+        nc.scalar.dma_start(out=gb_rows[8:16, :], in_=ln_b.rearrange("(c p) -> c p", p=P))
+        fcw_sb = const.tile([P, H2], BF16)
+        nc.scalar.dma_start(out=fcw_sb[:], in_=fc_W)
+        fcb_bf = const.tile([P, D_OUT], BF16)
+        nc.scalar.dma_start(out=fcb_bf[:], in_=fc_b.partition_broadcast(P))
+
+        ident_f = const.tile([P, P], F32)
+        make_identity(nc, ident_f[:])
+        ident_b = const.tile([P, P], BF16)
+        make_identity(nc, ident_b[:])
+        neg_half = const.tile([P, ROW_TILES], F32)
+        nc.vector.memset(neg_half[:], -0.5)
+
+        warm = const.tile([P, 1], F32)
+        nc.vector.memset(warm[:], 0.0)
+        nc.scalar.activation(out=warm[:], in_=warm[:], func=ACT.Tanh)
+
+        st = {}
+
+        def a_transposes(key, src, half, tag, bufs):
+            s32 = src[:].bitcast(F32)
+            hT_ps = psum.tile([P, 4, P], F32, name="hT_ps", tag=tag, bufs=bufs)
+            for i2 in range(2):
+                for u in range(2):
+                    col = 256 * (2 * half + i2) + 128 * u
+                    nc.tensor.transpose(
+                        hT_ps[:, 2 * i2 + u, :], s32[:, col : col + 128], ident_f[:]
+                    )
+            st[(key, "hT")] = hT_ps
+
+        def a_exit(key, on_scalar):
+            grouped = work.tile([P, 2 * H], BF16, align_bytes=64, name="grouped_h", bufs=4)
+            dst = grouped[:].bitcast(F32).rearrange("p (i r u) -> p i r u", i=2, u=2)
+            src = st[(key, "hT")][:].rearrange("p (i u) r -> p i r u", u=2)
+            if on_scalar:
+                nc.scalar.copy(out=dst, in_=src)
+            else:
+                nc.vector.tensor_copy(out=dst, in_=src)
+            st[(key, "grouped")] = grouped
+
+        def a_quantise(key, codes, scales):
+            nc.vector.quantize_mx(
+                out=codes.bitcast(FP8X4), scales=scales, in_=st[(key, "grouped")][:]
+            )
+
+        w_codes = const.tile([P, H], U32, align_bytes=64)
+        w_scales = const.tile([P, H], U8, align_bytes=64)
+        for half in range(2):
+            a_transposes(("w", half), w_sb, half, "xT", 4)
+        for half in range(2):
+            a_exit(("w", half), half == 1)
+        for half in range(2):
+            cols = slice(256 * half, 256 * half + 256)
+            a_quantise(("w", half), w_codes[:, cols], w_scales[:, cols])
+
+        bias_bc = const.tile([P, H], F32)
+        fcb_bc = const.tile([P, ROW_TILES * D_OUT], F32)
+        f_codes = const.tile([P, 2 * D_OUT], U32, align_bytes=64)
+        f_scales = const.tile([P, 2 * D_OUT], U8, align_bytes=64)
+        gb_col = const.tile([P, 16], F32)
+
+        def setup_bias():
+            nc.vector.tensor_tensor(out=bias_bc[:], in0=b1_bc[:], in1=b2_bc[:], op=ALU.add)
+
+        def setup_second_stage():
+            gb_ps = psum.tile([P, P], BF16, name="gb_ps", tag="o", bufs=1)
+            nc.tensor.transpose(gb_ps[:], gb_rows[:], ident_b[:])
+            nc.vector.tensor_copy(out=gb_col[:], in_=gb_ps[:, 0:16])
+            fT_ps = psum.tile([P, 8, P], BF16, name="fT_ps", tag="o", bufs=1)
+            for c in range(8):
+                nc.tensor.transpose(fT_ps[:, c, :], fcw_sb[:, c * P : (c + 1) * P], ident_b[:])
+            grouped_f = const.tile([P, H2], BF16, align_bytes=64)
+            nc.vector.tensor_copy(
+                out=grouped_f[:].rearrange("p (h c j) -> p h c j", h=2, j=4),
+                in_=fT_ps[:].rearrange("p (h j) c -> p h c j", j=4),
+            )
+            for i in range(ROW_TILES):
+                nc.vector.tensor_copy(
+                    out=fcb_bc[:, i * D_OUT : (i + 1) * D_OUT], in_=fcb_bf[:]
+                )
+            nc.vector.quantize_mx(
+                out=f_codes[:].bitcast(FP8X4), scales=f_scales[:], in_=grouped_f[:]
+            )
+
+        def ok(b):
+            return 0 <= b < N_BLOCKS
+
+        def b_matmul(b, i):
+            cols = slice((i % 2) * P, (i % 2 + 1) * P)
+            z_ps = psum.tile([P, H], F32, name="z_ps", tag="z", bufs=2)
+            nc.tensor.matmul_mx(
+                out=z_ps[:],
+                lhsT=st[(2 * b + i // 2, "codes")][:, cols].bitcast(FP8X4),
+                lhsT_scale=st[(2 * b + i // 2, "scales")][:, cols],
+                rhs=w_codes[:].bitcast(FP8X4),
+                rhs_scale=w_scales[:],
+                start=True,
+                stop=True,
+            )
+            st[(b, "z", i)] = z_ps
+
+        def b_add(b, i):
+            zb = acts.tile([P, H], F32, name="zb", bufs=4)
+            nc.vector.tensor_tensor(
+                out=zb[:], in0=st[(b, "z", i)][:], in1=bias_bc[:], op=ALU.add
+            )
+            st[(b, "zb", i)] = zb
+
+        def b_act(b, i):
+            if i == 0:
+                st[(b, "s1")] = small.tile([P, ROW_TILES], F32, name="s1")
+                st[(b, "s2")] = small.tile([P, ROW_TILES], F32, name="s2")
+            h2 = acts.tile([P, H], F32, name="h2")
+            nc.scalar.activation(
+                out=h2[:], in_=st[(b, "zb", i)][:], func=ACT.Tanh,
+                accum_out=st[(b, "s1")][:, i : i + 1],
+            )
+            junk = work.tile([P, H], BF16, name="junk")
+            nc.scalar.activation(
+                out=junk[:], in_=h2[:], func=ACT.Square,
+                accum_out=st[(b, "s2")][:, i : i + 1],
+            )
+            st[(b, "h2", i)] = h2
+
+        def b_stats(b, half):
+            if half == 0:
+                for nm in ("neg_mean", "ex2", "msq", "var_eps", "rstd"):
+                    st[(b, nm)] = small.tile([P, ROW_TILES], F32, name=nm)
+            c = slice(2 * half, 2 * half + 2)
+            nc.gpsimd.tensor_scalar(
+                out=st[(b, "neg_mean")][:, c], in0=st[(b, "s1")][:, c],
+                scalar1=-1.0 / H, scalar2=0.0, op0=ALU.mult, op1=ALU.add,
+            )
+            nc.gpsimd.tensor_scalar(
+                out=st[(b, "ex2")][:, c], in0=st[(b, "s2")][:, c],
+                scalar1=1.0 / H, scalar2=LN_EPS, op0=ALU.mult, op1=ALU.add,
+            )
+            nc.gpsimd.tensor_tensor(
+                out=st[(b, "msq")][:, c], in0=st[(b, "neg_mean")][:, c],
+                in1=st[(b, "neg_mean")][:, c], op=ALU.mult,
+            )
+            nc.gpsimd.tensor_tensor(
+                out=st[(b, "var_eps")][:, c], in0=st[(b, "ex2")][:, c],
+                in1=st[(b, "msq")][:, c], op=ALU.subtract,
+            )
+            nc.gpsimd.tensor_tensor(
+                out=st[(b, "rstd")][:, c], in0=st[(b, "var_eps")][:, c],
+                in1=neg_half[:, c], op=ALU.pow,
+            )
+
+        def b_xhat(b, i):
+            xh = acts.tile([P, H], F32, name="xh")
+            eng = nc.gpsimd if XH_ON_GPSIMD else nc.vector
+            eng.tensor_scalar(
+                out=xh[:], in0=st[(b, "h2", i)][:],
+                scalar1=st[(b, "neg_mean")][:, i : i + 1],
+                scalar2=st[(b, "rstd")][:, i : i + 1],
+                op0=ALU.add, op1=ALU.mult,
+            )
+            st[(b, "xh", i)] = xh
+
+        def c_transposes(b, t):
+            xT_ps = psum.tile([P, BLOCK], F32, name="xT_ps", tag="xT", bufs=4)
+            for i in range(ROW_TILES):
+                nc.tensor.transpose(
+                    xT_ps[:, i * P : (i + 1) * P],
+                    st[(b, "xh", i)][:, t * P : (t + 1) * P],
+                    ident_f[:],
+                )
+            st[(b, "xT", t)] = xT_ps
+
+        def planes_of(b, h):
+            if (b, "planes", h) not in st:
+                st[(b, "planes", h)] = work.tile([P, 4, BLOCK], BF16, name="planes%d" % h)
+            return st[(b, "planes", h)]
+
+        def vector_empties(b, t):
+            return t == 3 and b % 2 == 1
+
+        def c_exit(b, h, t, on_vector):
+            c = 4 * h + t
+            if on_vector:
+                nc.vector.tensor_scalar(
+                    out=planes_of(b, h)[:, t, :], in0=st[(b, "xT", t)][:],
+                    scalar1=gb_col[:, c : c + 1], scalar2=gb_col[:, 8 + c : 9 + c],
+                    op0=ALU.mult, op1=ALU.add,
+                )
+            else:
+                nc.scalar.activation(
+                    out=planes_of(b, h)[:, t, :], in_=st[(b, "xT", t)][:], func=ACT.Identity,
+                    scale=gb_col[:, c : c + 1], bias=gb_col[:, 8 + c : 9 + c],
+                )
+
+        def c_regroup(b, h):
+            grouped_n = work.tile([P, BLOCK, 4], BF16, align_bytes=64, name="grouped_n%d" % h)
+            nc.vector.tensor_copy(
+                out=grouped_n[:].rearrange("p (c i) t -> p c t i", i=4),
+                in_=st[(b, "planes", h)][:].rearrange("p t (c i) -> p c t i", i=4),
+            )
+            st[(b, "grouped_n", h)] = grouped_n
+
+        def c_quantise(b, h):
+            codes = work.tile([P, BLOCK], U32, align_bytes=64, name="n_codes%d" % h)
+            scales = work.tile([P, BLOCK], U8, align_bytes=64, name="n_scales%d" % h)
+            nc.vector.quantize_mx(
+                out=codes[:].bitcast(FP8X4), scales=scales[:],
+                in_=st[(b, "grouped_n", h)][:].rearrange("p c t -> p (c t)"),
+            )
+            st[(b, "n_codes", h)] = codes
+            st[(b, "n_scales", h)] = scales
+
+        def d_matmuls(b):
+            o_ps = psum.tile([P, ROW_TILES * D_OUT], F32, name="o_ps", tag="o", bufs=1)
+            for i in range(ROW_TILES):
+                cols = slice(i * P, (i + 1) * P)
+                for h in range(2):
+                    nc.tensor.matmul_mx(
+                        out=o_ps[:, i * D_OUT : (i + 1) * D_OUT],
+                        lhsT=st[(b, "n_codes", h)][:, cols].bitcast(FP8X4),
+                        lhsT_scale=st[(b, "n_scales", h)][:, cols],
+                        rhs=f_codes[:, h * D_OUT : (h + 1) * D_OUT].bitcast(FP8X4),
+                        rhs_scale=f_scales[:, h * D_OUT : (h + 1) * D_OUT],
+                        start=(h == 0),
+                        stop=(h == 1),
+                    )
+            st[(b, "o")] = o_ps
+
+        def d_store(b):
+            o_sb = work.tile([P, ROW_TILES * D_OUT], F32, name="o_sb", bufs=3)
+            nc.vector.tensor_tensor(out=o_sb[:], in0=st[(b, "o")][:], in1=fcb_bc[:], op=ALU.add)
+            nc.sync.dma_start(
+                out=out[b * BLOCK : (b + 1) * BLOCK, :].rearrange(
+                    "(p i) c -> p (i c)", i=ROW_TILES
+                ),
+                in_=o_sb[:],
+            )
+
+        def every(slot, lag, size, count):
+            index, rest = divmod(slot - lag, size)
+            return index if rest == 0 and 0 <= index < count else None
+
+        n_rows = 4 * N_BLOCKS
+        n_halves = 2 * N_BLOCKS
+        for slot in range(-10, n_rows + 8):
+            if slot == -7:
+                setup_bias()
+            if slot == -2:
+                setup_second_stage()
+            r = every(slot, -7, 1, n_rows)
+            if r is not None:
+                b_matmul(r // 4, r % 4)
+            b = every(slot, 10, 4, N_BLOCKS)
+            if b is not None:
+                d_matmuls(b)
+            b = every(slot, 3, 4, N_BLOCKS)
+            if b is not None:
+                for t in range(4):
+                    c_transposes(b, t)
+            hb = every(slot, -10, 2, n_halves)
+            if hb is not None:
+                a_transposes(hb, h1_tiles[hb // 2], hb % 2, "hT", 1)
+            r = every(slot, -6, 1, n_rows)
+            if r is not None:
+                b_add(r // 4, r % 4)
+            hb = every(slot, -8, 2, n_halves)
+            if hb is not None:
+                st[(hb, "codes")] = work.tile(
+                    [P, 2 * P], U32, align_bytes=64, name="h_codes", bufs=4
+                )
+                st[(hb, "scales")] = work.tile(
+                    [P, 2 * P], U8, align_bytes=64, name="h_scales", bufs=4
+                )
+                a_quantise(hb, st[(hb, "codes")][:], st[(hb, "scales")][:])
+            b = every(slot, 6, 4, N_BLOCKS)
+            if b is not None and vector_empties(b, 3):
+                c_exit(b, 0, 3, True)
+                c_exit(b, 1, 3, True)
+            hb = every(slot, -9, 2, n_halves)
+            if hb is not None:
+                a_exit(hb, False)
+            hb = every(slot, 6, 2, n_halves)
+            if hb is not None:
+                c_regroup(hb // 2, hb % 2)
+            hb = every(slot, 7, 2, n_halves)
+            if hb is not None:
+                c_quantise(hb // 2, hb % 2)
+            b = every(slot, 11, 4, N_BLOCKS)
+            if b is not None:
+                d_store(b)
+            r = every(slot, -4, 1, n_rows)
+            if r is not None:
+                b_act(r // 4, r % 4)
+            e = every(slot, 3, 1, n_rows)
+            if e is not None:
+                for t in (2 * (e % 2), 2 * (e % 2) + 1):
+                    if not vector_empties(e // 4, t):
+                        c_exit(e // 4, (e % 4) // 2, t, False)
+            hb = every(slot, -3, 2, n_halves)
+            if hb is not None:
+                b_stats(hb // 2, hb % 2)
+                b_xhat(hb // 2, 2 * (hb % 2))
+                b_xhat(hb // 2, 2 * (hb % 2) + 1)

@@ -19,7 +19,7 @@ BLOCK = P * ROW_TILES
 N_BLOCKS = B // BLOCK
 FLOPS = 2 * B * H * H + 2 * B * H2 * D_OUT
 MANUAL = True
-XH_ON_GPSIMD = True
+XH_ON_GPSIMD = False
 
 
 def tile_rnnclassifier_pa_t_kernel(
@@ -235,7 +235,7 @@ def tile_rnnclassifier_pa_t_kernel(
             return st[(b, "planes", h)]
 
         def vector_empties(b, t):
-            return t == 3 and b % 2 == 1
+            return False
 
         def c_exit(b, h, t, on_vector):
             c = 4 * h + t
@@ -301,7 +301,7 @@ def tile_rnnclassifier_pa_t_kernel(
 
         n_rows = 4 * N_BLOCKS
         n_halves = 2 * N_BLOCKS
-        for slot in range(-10, n_rows + 8):
+        for slot in range(-10, n_rows + 10):
             if slot == -7:
                 setup_bias()
             if slot == -2:
@@ -309,10 +309,10 @@ def tile_rnnclassifier_pa_t_kernel(
             r = every(slot, -7, 1, n_rows)
             if r is not None:
                 b_matmul(r // 4, r % 4)
-            b = every(slot, 10, 4, N_BLOCKS)
+            b = every(slot, 12, 4, N_BLOCKS)
             if b is not None:
                 d_matmuls(b)
-            b = every(slot, 3, 4, N_BLOCKS)
+            b = every(slot, 5, 4, N_BLOCKS)
             if b is not None:
                 for t in range(4):
                     c_transposes(b, t)
@@ -322,6 +322,10 @@ def tile_rnnclassifier_pa_t_kernel(
             r = every(slot, -6, 1, n_rows)
             if r is not None:
                 b_add(r // 4, r % 4)
+            hb = every(slot, 1, 2, n_halves)
+            if hb is not None:
+                b_xhat(hb // 2, 2 * (hb % 2))
+                b_xhat(hb // 2, 2 * (hb % 2) + 1)
             hb = every(slot, -8, 2, n_halves)
             if hb is not None:
                 st[(hb, "codes")] = work.tile(
@@ -331,26 +335,26 @@ def tile_rnnclassifier_pa_t_kernel(
                     [P, 2 * P], U8, align_bytes=64, name="h_scales", bufs=4
                 )
                 a_quantise(hb, st[(hb, "codes")][:], st[(hb, "scales")][:])
-            b = every(slot, 6, 4, N_BLOCKS)
+            b = every(slot, 8, 4, N_BLOCKS)
             if b is not None and vector_empties(b, 3):
                 c_exit(b, 0, 3, True)
                 c_exit(b, 1, 3, True)
             hb = every(slot, -9, 2, n_halves)
             if hb is not None:
                 a_exit(hb, False)
-            hb = every(slot, 6, 2, n_halves)
+            hb = every(slot, 8, 2, n_halves)
             if hb is not None:
                 c_regroup(hb // 2, hb % 2)
-            hb = every(slot, 7, 2, n_halves)
+            hb = every(slot, 9, 2, n_halves)
             if hb is not None:
                 c_quantise(hb // 2, hb % 2)
-            b = every(slot, 11, 4, N_BLOCKS)
+            b = every(slot, 13, 4, N_BLOCKS)
             if b is not None:
                 d_store(b)
             r = every(slot, -4, 1, n_rows)
             if r is not None:
                 b_act(r // 4, r % 4)
-            e = every(slot, 3, 1, n_rows)
+            e = every(slot, 5, 1, n_rows)
             if e is not None:
                 for t in (2 * (e % 2), 2 * (e % 2) + 1):
                     if not vector_empties(e // 4, t):
@@ -358,5 +362,3 @@ def tile_rnnclassifier_pa_t_kernel(
             hb = every(slot, -3, 2, n_halves)
             if hb is not None:
                 b_stats(hb // 2, hb % 2)
-                b_xhat(hb // 2, 2 * (hb % 2))
-                b_xhat(hb // 2, 2 * (hb % 2) + 1)

@@ -18,7 +18,7 @@ ROW_TILES = 4
 BLOCK = P * ROW_TILES
 N_BLOCKS = B // BLOCK
 FLOPS = 2 * B * H * H + 2 * B * H2 * D_OUT
-MANUAL = True
+MANUAL = False
 XH_ON_GPSIMD = False
 
 

@@ -235,7 +235,7 @@ def tile_rnnclassifier_pa_t_kernel(
             return st[(b, "planes", h)]
 
         def vector_empties(b, t):
-            return False
+            return t == 3 and b % 4 == 1
 
         def c_exit(b, h, t, on_vector):
             c = 4 * h + t
@@ -335,10 +335,6 @@ def tile_rnnclassifier_pa_t_kernel(
                     [P, 2 * P], U8, align_bytes=64, name="h_scales", bufs=4
                 )
                 a_quantise(hb, st[(hb, "codes")][:], st[(hb, "scales")][:])
-            b = every(slot, 8, 4, N_BLOCKS)
-            if b is not None and vector_empties(b, 3):
-                c_exit(b, 0, 3, True)
-                c_exit(b, 1, 3, True)
             hb = every(slot, -9, 2, n_halves)
             if hb is not None:
                 a_exit(hb, False)
@@ -357,8 +353,7 @@ def tile_rnnclassifier_pa_t_kernel(
             e = every(slot, 5, 1, n_rows)
             if e is not None:
                 for t in (2 * (e % 2), 2 * (e % 2) + 1):
-                    if not vector_empties(e // 4, t):
-                        c_exit(e // 4, (e % 4) // 2, t, False)
+                    c_exit(e // 4, (e % 4) // 2, t, vector_empties(e // 4, t))
             hb = every(slot, -3, 2, n_halves)
             if hb is not None:
                 b_stats(hb // 2, hb % 2)

@@ -148,15 +148,16 @@ def tile_rnnclassifier_pa_t_kernel(
         def b_matmul(b, i):
             cols = slice((i % 2) * P, (i % 2 + 1) * P)
             z_ps = psum.tile([P, H], F32, name="z_ps", tag="z", bufs=2)
-            nc.tensor.matmul_mx(
-                out=z_ps[:],
-                lhsT=st[(2 * b + i // 2, "codes")][:, cols].bitcast(FP8X4),
-                lhsT_scale=st[(2 * b + i // 2, "scales")][:, cols],
-                rhs=w_codes[:].bitcast(FP8X4),
-                rhs_scale=w_scales[:],
-                start=True,
-                stop=True,
-            )
+            for rep in range(2):
+                nc.tensor.matmul_mx(
+                    out=z_ps[:],
+                    lhsT=st[(2 * b + i // 2, "codes")][:, cols].bitcast(FP8X4),
+                    lhsT_scale=st[(2 * b + i // 2, "scales")][:, cols],
+                    rhs=w_codes[:].bitcast(FP8X4),
+                    rhs_scale=w_scales[:],
+                    start=True,
+                    stop=True,
+                )
             st[(b, "z", i)] = z_ps
 
         def b_add(b, i):

@@ -31,7 +31,7 @@ def tile_rnnclassifier_pa_t_kernel(
             stack.enter_context(tc.manual_schedule())
         const = stack.enter_context(tc.tile_pool(name="const", bufs=1))
         h1pool = stack.enter_context(tc.tile_pool(name="h1pool", bufs=N_BLOCKS))
-        work = stack.enter_context(tc.tile_pool(name="work", bufs=2))
+        work = stack.enter_context(tc.tile_pool(name="work", bufs=3))
         acts = stack.enter_context(tc.tile_pool(name="acts", bufs=8))
         small = stack.enter_context(tc.tile_pool(name="small", bufs=4))
         psum = stack.enter_context(tc.psum_pool(name="psum", bufs=1))
@@ -148,20 +148,19 @@ def tile_rnnclassifier_pa_t_kernel(
         def b_matmul(b, i):
             cols = slice((i % 2) * P, (i % 2 + 1) * P)
             z_ps = psum.tile([P, H], F32, name="z_ps", tag="z", bufs=2)
-            for rep in range(2):
-                nc.tensor.matmul_mx(
-                    out=z_ps[:],
-                    lhsT=st[(2 * b + i // 2, "codes")][:, cols].bitcast(FP8X4),
-                    lhsT_scale=st[(2 * b + i // 2, "scales")][:, cols],
-                    rhs=w_codes[:].bitcast(FP8X4),
-                    rhs_scale=w_scales[:],
-                    start=True,
-                    stop=True,
-                )
+            nc.tensor.matmul_mx(
+                out=z_ps[:],
+                lhsT=st[(2 * b + i // 2, "codes")][:, cols].bitcast(FP8X4),
+                lhsT_scale=st[(2 * b + i // 2, "scales")][:, cols],
+                rhs=w_codes[:].bitcast(FP8X4),
+                rhs_scale=w_scales[:],
+                start=True,
+                stop=True,
+            )
             st[(b, "z", i)] = z_ps
 
         def b_add(b, i):
-            zb = acts.tile([P, H], F32, name="zb", bufs=4)
+            zb = acts.tile([P, H], F32, name="zb", bufs=8)
             nc.vector.tensor_tensor(
                 out=zb[:], in0=st[(b, "z", i)][:], in1=bias_bc[:], op=ALU.add
             )
@@ -236,7 +235,7 @@ def tile_rnnclassifier_pa_t_kernel(
             return st[(b, "planes", h)]
 
         def vector_empties(b, t):
-            return t == 3 and b % 4 == 1
+            return False
 
         def c_exit(b, h, t, on_vector):
             c = 4 * h + t
@@ -336,6 +335,10 @@ def tile_rnnclassifier_pa_t_kernel(
                     [P, 2 * P], U8, align_bytes=64, name="h_scales", bufs=4
                 )
                 a_quantise(hb, st[(hb, "codes")][:], st[(hb, "scales")][:])
+            b = every(slot, 8, 4, N_BLOCKS)
+            if b is not None and vector_empties(b, 3):
+                c_exit(b, 0, 3, True)
+                c_exit(b, 1, 3, True)
             hb = every(slot, -9, 2, n_halves)
             if hb is not None:
                 a_exit(hb, False)
@@ -354,7 +357,8 @@ def tile_rnnclassifier_pa_t_kernel(
             e = every(slot, 5, 1, n_rows)
             if e is not None:
                 for t in (2 * (e % 2), 2 * (e % 2) + 1):
-                    c_exit(e // 4, (e % 4) // 2, t, vector_empties(e // 4, t))
+                    if not vector_empties(e // 4, t):
+                        c_exit(e // 4, (e % 4) // 2, t, False)
             hb = every(slot, -3, 2, n_halves)
             if hb is not None:
                 b_stats(hb // 2, hb % 2)

@@ -31,7 +31,7 @@ def tile_rnnclassifier_pa_t_kernel(
             stack.enter_context(tc.manual_schedule())
         const = stack.enter_context(tc.tile_pool(name="const", bufs=1))
         h1pool = stack.enter_context(tc.tile_pool(name="h1pool", bufs=N_BLOCKS))
-        work = stack.enter_context(tc.tile_pool(name="work", bufs=3))
+        work = stack.enter_context(tc.tile_pool(name="work", bufs=2))
         acts = stack.enter_context(tc.tile_pool(name="acts", bufs=8))
         small = stack.enter_context(tc.tile_pool(name="small", bufs=4))
         psum = stack.enter_context(tc.psum_pool(name="psum", bufs=1))
@@ -160,7 +160,7 @@ def tile_rnnclassifier_pa_t_kernel(
             st[(b, "z", i)] = z_ps
 
         def b_add(b, i):
-            zb = acts.tile([P, H], F32, name="zb", bufs=8)
+            zb = acts.tile([P, H], F32, name="zb", bufs=4)
             nc.vector.tensor_tensor(
                 out=zb[:], in0=st[(b, "z", i)][:], in1=bias_bc[:], op=ALU.add
             )
@@ -182,11 +182,10 @@ def tile_rnnclassifier_pa_t_kernel(
             )
             st[(b, "h2", i)] = h2
 
-        def b_stats(b, half):
-            if half == 0:
-                for nm in ("neg_mean", "ex2", "msq", "var_eps", "rstd"):
-                    st[(b, nm)] = small.tile([P, ROW_TILES], F32, name=nm)
-            c = slice(2 * half, 2 * half + 2)
+        def b_stats(b):
+            for nm in ("neg_mean", "ex2", "msq", "var_eps", "rstd"):
+                st[(b, nm)] = small.tile([P, ROW_TILES], F32, name=nm)
+            c = slice(0, ROW_TILES)
             nc.gpsimd.tensor_scalar(
                 out=st[(b, "neg_mean")][:, c], in0=st[(b, "s1")][:, c],
                 scalar1=-1.0 / H, scalar2=0.0, op0=ALU.mult, op1=ALU.add,
@@ -359,6 +358,6 @@ def tile_rnnclassifier_pa_t_kernel(
                 for t in (2 * (e % 2), 2 * (e % 2) + 1):
                     if not vector_empties(e // 4, t):
                         c_exit(e // 4, (e % 4) // 2, t, False)
-            hb = every(slot, -3, 2, n_halves)
-            if hb is not None:
-                b_stats(hb // 2, hb % 2)
+            b = every(slot, -1, 4, N_BLOCKS)
+            if b is not None:
+                b_stats(b)

@@ -170,7 +170,7 @@ def tile_rnnclassifier_pa_t_kernel(
             if i == 0:
                 st[(b, "s1")] = small.tile([P, ROW_TILES], F32, name="s1")
                 st[(b, "s2")] = small.tile([P, ROW_TILES], F32, name="s2")
-            h2 = acts.tile([P, H], F32, name="h2")
+            h2 = acts.tile([P, H], F32, name="h2", bufs=12)
             nc.scalar.activation(
                 out=h2[:], in_=st[(b, "zb", i)][:], func=ACT.Tanh,
                 accum_out=st[(b, "s1")][:, i : i + 1],
@@ -182,10 +182,11 @@ def tile_rnnclassifier_pa_t_kernel(
             )
             st[(b, "h2", i)] = h2
 
-        def b_stats(b):
-            for nm in ("neg_mean", "ex2", "msq", "var_eps", "rstd"):
-                st[(b, nm)] = small.tile([P, ROW_TILES], F32, name=nm)
-            c = slice(0, ROW_TILES)
+        def b_stats(b, half):
+            if half == 0:
+                for nm in ("neg_mean", "ex2", "msq", "var_eps", "rstd"):
+                    st[(b, nm)] = small.tile([P, ROW_TILES], F32, name=nm)
+            c = slice(2 * half, 2 * half + 2)
             nc.gpsimd.tensor_scalar(
                 out=st[(b, "neg_mean")][:, c], in0=st[(b, "s1")][:, c],
                 scalar1=-1.0 / H, scalar2=0.0, op0=ALU.mult, op1=ALU.add,
@@ -300,7 +301,7 @@ def tile_rnnclassifier_pa_t_kernel(
 
         n_rows = 4 * N_BLOCKS
         n_halves = 2 * N_BLOCKS
-        for slot in range(-10, n_rows + 10):
+        for slot in range(-10, n_rows + 12):
             if slot == -7:
                 setup_bias()
             if slot == -2:
@@ -308,10 +309,10 @@ def tile_rnnclassifier_pa_t_kernel(
             r = every(slot, -7, 1, n_rows)
             if r is not None:
                 b_matmul(r // 4, r % 4)
-            b = every(slot, 12, 4, N_BLOCKS)
+            b = every(slot, 14, 4, N_BLOCKS)
             if b is not None:
                 d_matmuls(b)
-            b = every(slot, 5, 4, N_BLOCKS)
+            b = every(slot, 7, 4, N_BLOCKS)
             if b is not None:
                 for t in range(4):
                     c_transposes(b, t)
@@ -321,7 +322,7 @@ def tile_rnnclassifier_pa_t_kernel(
             r = every(slot, -6, 1, n_rows)
             if r is not None:
                 b_add(r // 4, r % 4)
-            hb = every(slot, 1, 2, n_halves)
+            hb = every(slot, 3, 2, n_halves)
             if hb is not None:
                 b_xhat(hb // 2, 2 * (hb % 2))
                 b_xhat(hb // 2, 2 * (hb % 2) + 1)
@@ -341,23 +342,23 @@ def tile_rnnclassifier_pa_t_kernel(
             hb = every(slot, -9, 2, n_halves)
             if hb is not None:
                 a_exit(hb, False)
-            hb = every(slot, 8, 2, n_halves)
+            hb = every(slot, 10, 2, n_halves)
             if hb is not None:
                 c_regroup(hb // 2, hb % 2)
-            hb = every(slot, 9, 2, n_halves)
+            hb = every(slot, 11, 2, n_halves)
             if hb is not None:
                 c_quantise(hb // 2, hb % 2)
-            b = every(slot, 13, 4, N_BLOCKS)
+            b = every(slot, 15, 4, N_BLOCKS)
             if b is not None:
                 d_store(b)
             r = every(slot, -4, 1, n_rows)
             if r is not None:
                 b_act(r // 4, r % 4)
-            e = every(slot, 5, 1, n_rows)
+            e = every(slot, 7, 1, n_rows)
             if e is not None:
                 for t in (2 * (e % 2), 2 * (e % 2) + 1):
                     if not vector_empties(e // 4, t):
                         c_exit(e // 4, (e % 4) // 2, t, False)
-            b = every(slot, -1, 4, N_BLOCKS)
-            if b is not None:
-                b_stats(b)
+            hb = every(slot, -3, 2, n_halves)
+            if hb is not None:
+                b_stats(hb // 2, hb % 2)

from contextlib import ExitStack

from concourse import mybir
from concourse.masks import make_identity

F32 = mybir.dt.float32
BF16 = mybir.dt.bfloat16
U32 = mybir.dt.uint32
U8 = mybir.dt.uint8
FP8X4 = mybir.dt.float8_e4m3fn_x4
ACT = mybir.ActivationFunctionType
ALU = mybir.AluOpType

P = 128
B, H, H2, D_OUT = 8192, 512, 1024, 128
LN_EPS = 1e-5
ROW_TILES = 4
BLOCK = P * ROW_TILES
N_BLOCKS = B // BLOCK
FLOPS = 2 * B * H * H + 2 * B * H2 * D_OUT
MANUAL = False
XH_ON_GPSIMD = False


def tile_rnnclassifier_pa_t_kernel(
    tc, h1, W_ih1, b_ih1, b_hh1, ln_g, ln_b, fc_W, fc_b, out
):
    nc = tc.nc
    with ExitStack() as stack:
        if MANUAL:
            stack.enter_context(tc.manual_schedule())
        const = stack.enter_context(tc.tile_pool(name="const", bufs=1))
        h1pool = stack.enter_context(tc.tile_pool(name="h1pool", bufs=N_BLOCKS))
        work = stack.enter_context(tc.tile_pool(name="work", bufs=2))
        acts = stack.enter_context(tc.tile_pool(name="acts", bufs=8))
        small = stack.enter_context(tc.tile_pool(name="small", bufs=4))
        psum = stack.enter_context(tc.psum_pool(name="psum", bufs=1))

        w_sb = const.tile([P, 4 * H], BF16)
        nc.sync.dma_start(
            out=w_sb[:].rearrange("p (t k) -> p t k", t=4),
            in_=W_ih1.rearrange("(t p) k -> p t k", p=P),
        )
        h1_tiles = []
        for blk in range(N_BLOCKS):
            h1_sb = h1pool.tile([P, ROW_TILES * H], BF16, name="h1_sb")
            nc.sync.dma_start(
                out=h1_sb[:],
                in_=h1[blk * BLOCK : (blk + 1) * BLOCK, :].rearrange(
                    "(p i) k -> p (i k)", i=ROW_TILES
                ),
            )
            h1_tiles.append(h1_sb)
        b1_bc = const.tile([P, H], BF16)
        nc.scalar.dma_start(out=b1_bc[:], in_=b_ih1.partition_broadcast(P))
        b2_bc = const.tile([P, H], BF16)
        nc.scalar.dma_start(out=b2_bc[:], in_=b_hh1.partition_broadcast(P))
        gb_rows = const.tile([P, P], BF16)
        nc.vector.memset(gb_rows[:], 0.0)
        nc.scalar.dma_start(out=gb_rows[0:8, :], in_=ln_g.rearrange("(c p) -> c p", p=P))
        nc.scalar.dma_start(out=gb_rows[8:16, :], in_=ln_b.rearrange("(c p) -> c p", p=P))
        fcw_sb = const.tile([P, H2], BF16)
        nc.scalar.dma_start(out=fcw_sb[:], in_=fc_W)
        fcb_bf = const.tile([P, D_OUT], BF16)
        nc.scalar.dma_start(out=fcb_bf[:], in_=fc_b.partition_broadcast(P))

        ident_f = const.tile([P, P], F32)
        make_identity(nc, ident_f[:])
        ident_b = const.tile([P, P], BF16)
        make_identity(nc, ident_b[:])
        neg_half = const.tile([P, ROW_TILES], F32)
        nc.vector.memset(neg_half[:], -0.5)

        warm = const.tile([P, 1], F32)
        nc.vector.memset(warm[:], 0.0)
        nc.scalar.activation(out=warm[:], in_=warm[:], func=ACT.Tanh)

        st = {}

        def a_transposes(key, src, half, tag, bufs):
            s32 = src[:].bitcast(F32)
            hT_ps = psum.tile([P, 4, P], F32, name="hT_ps", tag=tag, bufs=bufs)
            for i2 in range(2):
                for u in range(2):
                    col = 256 * (2 * half + i2) + 128 * u
                    nc.tensor.transpose(
                        hT_ps[:, 2 * i2 + u, :], s32[:, col : col + 128], ident_f[:]
                    )
            st[(key, "hT")] = hT_ps

        def a_exit(key, on_scalar):
            grouped = work.tile([P, 2 * H], BF16, align_bytes=64, name="grouped_h", bufs=4)
            dst = grouped[:].bitcast(F32).rearrange("p (i r u) -> p i r u", i=2, u=2)
            src = st[(key, "hT")][:].rearrange("p (i u) r -> p i r u", u=2)
            if on_scalar:
                nc.scalar.copy(out=dst, in_=src)
            else:
                nc.vector.tensor_copy(out=dst, in_=src)
            st[(key, "grouped")] = grouped

        def a_quantise(key, codes, scales):
            nc.vector.quantize_mx(
                out=codes.bitcast(FP8X4), scales=scales, in_=st[(key, "grouped")][:]
            )

        w_codes = const.tile([P, H], U32, align_bytes=64)
        w_scales = const.tile([P, H], U8, align_bytes=64)
        for half in range(2):
            a_transposes(("w", half), w_sb, half, "xT", 4)
        for half in range(2):
            a_exit(("w", half), half == 1)
        for half in range(2):
            cols = slice(256 * half, 256 * half + 256)
            a_quantise(("w", half), w_codes[:, cols], w_scales[:, cols])

        bias_bc = const.tile([P, H], F32)
        fcb_bc = const.tile([P, ROW_TILES * D_OUT], F32)
        f_codes = const.tile([P, 2 * D_OUT], U32, align_bytes=64)
        f_scales = const.tile([P, 2 * D_OUT], U8, align_bytes=64)
        gb_col = const.tile([P, 16], F32)

        def setup_bias():
            nc.vector.tensor_tensor(out=bias_bc[:], in0=b1_bc[:], in1=b2_bc[:], op=ALU.add)

        def setup_second_stage():
            gb_ps = psum.tile([P, P], BF16, name="gb_ps", tag="o", bufs=1)
            nc.tensor.transpose(gb_ps[:], gb_rows[:], ident_b[:])
            nc.vector.tensor_copy(out=gb_col[:], in_=gb_ps[:, 0:16])
            fT_ps = psum.tile([P, 8, P], BF16, name="fT_ps", tag="o", bufs=1)
            for c in range(8):
                nc.tensor.transpose(fT_ps[:, c, :], fcw_sb[:, c * P : (c + 1) * P], ident_b[:])
            grouped_f = const.tile([P, H2], BF16, align_bytes=64)
            nc.vector.tensor_copy(
                out=grouped_f[:].rearrange("p (h c j) -> p h c j", h=2, j=4),
                in_=fT_ps[:].rearrange("p (h j) c -> p h c j", j=4),
            )
            for i in range(ROW_TILES):
                nc.vector.tensor_copy(
                    out=fcb_bc[:, i * D_OUT : (i + 1) * D_OUT], in_=fcb_bf[:]
                )
            nc.vector.quantize_mx(
                out=f_codes[:].bitcast(FP8X4), scales=f_scales[:], in_=grouped_f[:]
            )

        def ok(b):
            return 0 <= b < N_BLOCKS

        def b_matmul(b, i):
            cols = slice((i % 2) * P, (i % 2 + 1) * P)
            z_ps = psum.tile([P, H], F32, name="z_ps", tag="z", bufs=2)
            nc.tensor.matmul_mx(
                out=z_ps[:],
                lhsT=st[(2 * b + i // 2, "codes")][:, cols].bitcast(FP8X4),
                lhsT_scale=st[(2 * b + i // 2, "scales")][:, cols],
                rhs=w_codes[:].bitcast(FP8X4),
                rhs_scale=w_scales[:],
                start=True,
                stop=True,
            )
            st[(b, "z", i)] = z_ps

        def b_add(b, i):
            zb = acts.tile([P, H], F32, name="zb", bufs=4)
            nc.vector.tensor_tensor(
                out=zb[:], in0=st[(b, "z", i)][:], in1=bias_bc[:], op=ALU.add
            )
            st[(b, "zb", i)] = zb

        def b_act(b, i):
            if i == 0:
                st[(b, "s1")] = small.tile([P, ROW_TILES], F32, name="s1")
                st[(b, "s2")] = small.tile([P, ROW_TILES], F32, name="s2")
            h2 = acts.tile([P, H], F32, name="h2", bufs=12)
            nc.scalar.activation(
                out=h2[:], in_=st[(b, "zb", i)][:], func=ACT.Tanh,
                accum_out=st[(b, "s1")][:, i : i + 1],
            )
            junk = work.tile([P, H], BF16, name="junk")
            nc.scalar.activation(
                out=junk[:], in_=h2[:], func=ACT.Square,
                accum_out=st[(b, "s2")][:, i : i + 1],
            )
            st[(b, "h2", i)] = h2

        def b_stats(b, half):
            if half == 0:
                for nm in ("neg_mean", "ex2", "msq", "var_eps", "rstd"):
                    st[(b, nm)] = small.tile([P, ROW_TILES], F32, name=nm)
            c = slice(2 * half, 2 * half + 2)
            nc.gpsimd.tensor_scalar(
                out=st[(b, "neg_mean")][:, c], in0=st[(b, "s1")][:, c],
                scalar1=-1.0 / H, scalar2=0.0, op0=ALU.mult, op1=ALU.add,
            )
            nc.gpsimd.tensor_scalar(
                out=st[(b, "ex2")][:, c], in0=st[(b, "s2")][:, c],
                scalar1=1.0 / H, scalar2=LN_EPS, op0=ALU.mult, op1=ALU.add,
            )
            nc.gpsimd.tensor_tensor(
                out=st[(b, "msq")][:, c], in0=st[(b, "neg_mean")][:, c],
                in1=st[(b, "neg_mean")][:, c], op=ALU.mult,
            )
            nc.gpsimd.tensor_tensor(
                out=st[(b, "var_eps")][:, c], in0=st[(b, "ex2")][:, c],
                in1=st[(b, "msq")][:, c], op=ALU.subtract,
            )
            nc.gpsimd.tensor_tensor(
                out=st[(b, "rstd")][:, c], in0=st[(b, "var_eps")][:, c],
                in1=neg_half[:, c], op=ALU.pow,
            )

        def b_xhat(b, i):
            xh = acts.tile([P, H], F32, name="xh")
            eng = nc.gpsimd if XH_ON_GPSIMD else nc.vector
            eng.tensor_scalar(
                out=xh[:], in0=st[(b, "h2", i)][:],
                scalar1=st[(b, "neg_mean")][:, i : i + 1],
                scalar2=st[(b, "rstd")][:, i : i + 1],
                op0=ALU.add, op1=ALU.mult,
            )
            st[(b, "xh", i)] = xh

        def c_transposes(b, t):
            xT_ps = psum.tile([P, BLOCK], F32, name="xT_ps", tag="xT", bufs=4)
            for i in range(ROW_TILES):
                nc.tensor.transpose(
                    xT_ps[:, i * P : (i + 1) * P],
                    st[(b, "xh", i)][:, t * P : (t + 1) * P],
                    ident_f[:],
                )
            st[(b, "xT", t)] = xT_ps

        def planes_of(b, h):
            if (b, "planes", h) not in st:
                st[(b, "planes", h)] = work.tile([P, 4, BLOCK], BF16, name="planes%d" % h)
            return st[(b, "planes", h)]

        def vector_empties(b, t):
            return False

        def c_exit(b, h, t, on_vector):
            c = 4 * h + t
            if on_vector:
                nc.vector.tensor_scalar(
                    out=planes_of(b, h)[:, t, :], in0=st[(b, "xT", t)][:],
                    scalar1=gb_col[:, c : c + 1], scalar2=gb_col[:, 8 + c : 9 + c],
                    op0=ALU.mult, op1=ALU.add,
                )
            else:
                nc.scalar.activation(
                    out=planes_of(b, h)[:, t, :], in_=st[(b, "xT", t)][:], func=ACT.Identity,
                    scale=gb_col[:, c : c + 1], bias=gb_col[:, 8 + c : 9 + c],
                )

        def c_regroup(b, h):
            grouped_n = work.tile([P, BLOCK, 4], BF16, align_bytes=64, name="grouped_n%d" % h)
            nc.vector.tensor_copy(
                out=grouped_n[:].rearrange("p (c i) t -> p c t i", i=4),
                in_=st[(b, "planes", h)][:].rearrange("p t (c i) -> p c t i", i=4),
            )
            st[(b, "grouped_n", h)] = grouped_n

        def c_quantise(b, h):
            codes = work.tile([P, BLOCK], U32, align_bytes=64, name="n_codes%d" % h)
            scales = work.tile([P, BLOCK], U8, align_bytes=64, name="n_scales%d" % h)
            nc.vector.quantize_mx(
                out=codes[:].bitcast(FP8X4), scales=scales[:],
                in_=st[(b, "grouped_n", h)][:].rearrange("p c t -> p (c t)"),
            )
            st[(b, "n_codes", h)] = codes
            st[(b, "n_scales", h)] = scales

        def d_matmuls(b):
            o_ps = psum.tile([P, ROW_TILES * D_OUT], F32, name="o_ps", tag="o", bufs=1)
            for i in range(ROW_TILES):
                cols = slice(i * P, (i + 1) * P)
                for h in range(2):
                    nc.tensor.matmul_mx(
                        out=o_ps[:, i * D_OUT : (i + 1) * D_OUT],
                        lhsT=st[(b, "n_codes", h)][:, cols].bitcast(FP8X4),
                        lhsT_scale=st[(b, "n_scales", h)][:, cols],
                        rhs=f_codes[:, h * D_OUT : (h + 1) * D_OUT].bitcast(FP8X4),
                        rhs_scale=f_scales[:, h * D_OUT : (h + 1) * D_OUT],
                        start=(h == 0),
                        stop=(h == 1),
                    )
            st[(b, "o")] = o_ps

        def d_store(b):
            o_sb = work.tile([P, ROW_TILES * D_OUT], F32, name="o_sb", bufs=3)
            nc.vector.tensor_tensor(out=o_sb[:], in0=st[(b, "o")][:], in1=fcb_bc[:], op=ALU.add)
            nc.sync.dma_start(
                out=out[b * BLOCK : (b + 1) * BLOCK, :].rearrange(
                    "(p i) c -> p (i c)", i=ROW_TILES
                ),
                in_=o_sb[:],
            )

        def every(slot, lag, size, count):
            index, rest = divmod(slot - lag, size)
            return index if rest == 0 and 0 <= index < count else None

        n_rows = 4 * N_BLOCKS
        n_halves = 2 * N_BLOCKS
        for slot in range(-10, n_rows + 12):
            if slot == -7:
                setup_bias()
            if slot == -2:
                setup_second_stage()
            r = every(slot, -7, 1, n_rows)
            if r is not None:
                b_matmul(r // 4, r % 4)
            b = every(slot, 14, 4, N_BLOCKS)
            if b is not None:
                d_matmuls(b)
            b = every(slot, 7, 4, N_BLOCKS)
            if b is not None:
                for t in range(4):
                    c_transposes(b, t)
            hb = every(slot, -10, 2, n_halves)
            if hb is not None:
                a_transposes(hb, h1_tiles[hb // 2], hb % 2, "hT", 1)
            r = every(slot, -6, 1, n_rows)
            if r is not None:
                b_add(r // 4, r % 4)
            hb = every(slot, 3, 2, n_halves)
            if hb is not None:
                b_xhat(hb // 2, 2 * (hb % 2))
                b_xhat(hb // 2, 2 * (hb % 2) + 1)
            hb = every(slot, -8, 2, n_halves)
            if hb is not None:
                st[(hb, "codes")] = work.tile(
                    [P, 2 * P], U32, align_bytes=64, name="h_codes", bufs=4
                )
                st[(hb, "scales")] = work.tile(
                    [P, 2 * P], U8, align_bytes=64, name="h_scales", bufs=4
                )
                a_quantise(hb, st[(hb, "codes")][:], st[(hb, "scales")][:])
            b = every(slot, 8, 4, N_BLOCKS)
            if b is not None and vector_empties(b, 3):
                c_exit(b, 0, 3, True)
                c_exit(b, 1, 3, True)
            hb = every(slot, -9, 2, n_halves)
            if hb is not None:
                a_exit(hb, False)
            hb = every(slot, 10, 2, n_halves)
            if hb is not None:
                c_regroup(hb // 2, hb % 2)
            hb = every(slot, 11, 2, n_halves)
            if hb is not None:
                c_quantise(hb // 2, hb % 2)
            b = every(slot, 15, 4, N_BLOCKS)
            if b is not None:
                d_store(b)
            r = every(slot, -4, 1, n_rows)
            if r is not None:
                b_act(r // 4, r % 4)
            e = every(slot, 7, 1, n_rows)
            if e is not None:
                for t in (2 * (e % 2), 2 * (e % 2) + 1):
                    if not vector_empties(e // 4, t):
                        c_exit(e // 4, (e % 4) // 2, t, False)
            hb = every(slot, -3, 2, n_halves)
            if hb is not None:
                b_stats(hb // 2, hb % 2)
